import numpy as np
import ml_dtypes


def mxq(x, axis, fmt="e4m3"):
    dtype, down = {"e4m3": (ml_dtypes.float8_e4m3fn, 7), "e5m2": (ml_dtypes.float8_e5m2, 14)}[fmt]
    v = np.moveaxis(np.asarray(x, np.float32).astype(ml_dtypes.bfloat16).astype(np.float64), axis, -1)
    blocks = v.reshape(v.shape[:-1] + (-1, 32))
    amax = np.abs(blocks).max(-1, keepdims=True)
    byte = np.maximum(np.where(amax > 0, np.frexp(amax)[1] - 1 + 127, 0) - down, 1)
    scale = np.exp2(byte - 127.0)
    codes = (blocks / scale).astype(np.float32).astype(dtype).astype(np.float64)
    return np.moveaxis((codes * scale).reshape(v.shape), -1, axis)


WIDE = False


def mx_kscale(k):
    if not WIDE:
        return np.ones(k)
    levels = np.array([10, -10, 5, -5, 0])
    a = np.random.permutation(np.resize(levels, k // 512 * 4)).reshape(k // 512, 4)
    idx = np.arange(k)
    return np.exp2(a[idx // 512, idx % 128 // 32])


BF16 = ml_dtypes.bfloat16


def bf(x):
    return np.asarray(x, np.float32).astype(BF16)


def f64(x):
    return np.asarray(x).astype(np.float64)


E2M1 = np.array([0.0, 0.5, 1.0, 1.5, 2.0, 3.0, 4.0, 6.0, -0.0, -0.5, -1.0, -1.5, -2.0, -3.0, -4.0, -6.0])


def pack_weight(w, fmt):
    k, n = w.shape
    w = f64(bf(w)).reshape(k // 32, 32, n)
    amax = np.abs(w).max(1)
    if fmt == "e4m3":
        byte = np.frexp(amax)[1] - 1 + 127 - 7
    else:
        mant, ex = np.frexp(amax / 6.0)
        byte = np.where(mant > 0.5, ex, ex - 1) + 127
    byte = np.clip(np.where(amax > 0, byte, 1), 1, 254)
    scaled = (w * np.exp2(127.0 - byte)[:, None, :]).reshape(k, n).astype(np.float32)
    by_word = np.ascontiguousarray(scaled.reshape(k // 512, 128, 4, n).transpose(0, 1, 3, 2))
    if fmt == "e4m3":
        words = by_word.astype(ml_dtypes.float8_e4m3fn).view(np.uint8)
    else:
        c = by_word.astype(ml_dtypes.float4_e2m1fn).view(np.uint8) & 0xF
        words = c[..., 0::2] | (c[..., 1::2] << 4)
    return np.ascontiguousarray(words), np.ascontiguousarray(byte.astype(np.uint8).reshape(k // 512, 16, n))


def unpack_weight(words, scales, fmt):
    g, p, n, _ = words.shape
    if fmt == "e4m3":
        vals = np.ascontiguousarray(words).view(ml_dtypes.float8_e4m3fn).astype(np.float64)
    else:
        nib = np.empty((g, p, n, 4), np.uint8)
        nib[..., 0::2] = words & 0xF
        nib[..., 1::2] = words >> 4
        vals = E2M1[nib]
    vals = vals * np.repeat(np.exp2(scales.astype(np.float64) - 127.0), 8, axis=1)[..., None]
    return vals.transpose(0, 1, 3, 2).reshape(g * 512, n)

def pack4(w):
    words, scales = pack_weight(w, "e2m1")
    return words.reshape(words.shape[0], 128, -1), scales


def unpack4(words, scales):
    return unpack_weight(words.reshape(words.shape[0], 128, -1, 2), scales, "e2m1")


B, N, C, H, D = 1024, 9, 1024, 2, 64
MAX_FREQ = 10.0
BANDS = np.array([[1, 4], [4, 8], [8, 10], [10, 12], [12, 30], [30, 45], [1, 8], [8, 30], [1, 45]], dtype=np.float64)


def rotate_half(t):
    t2 = t.reshape(*t.shape[:-1], -1, 2)
    r = np.stack([-t2[..., 1], t2[..., 0]], axis=-1)
    return r.reshape(*t.shape)


def drofe_angles(head_dim):
    nf = head_dim // 4
    freqs = np.pi * np.linspace(1.0, MAX_FREQ / 2.0, nf)
    lo = BANDS[:, 0:1] * freqs
    hi = BANDS[:, 1:2] * freqs
    ang = np.concatenate([np.repeat(lo, 2, axis=-1), np.repeat(hi, 2, axis=-1)], axis=-1)
    return np.cos(ang), np.sin(ang)


def setup_inputs():
    s = mx_kscale(C)
    x = bf(np.random.standard_normal((B, N, C)) * s)
    demographic_info = bf(np.random.uniform(0.0, 1.0, (B, 2)))
    words, scales = pack4(np.random.standard_normal((C, 3 * H * D)) * 0.8 / np.sqrt(C) / s[:, None])
    return {"x": x,
            "demographic_info": demographic_info,
            "W_qkv_words": words,
            "W_qkv_scales": scales}


def reference(x, demographic_info, W_qkv_words, W_qkv_scales):
    y = mxq(f64(x), 2, "e4m3") @ unpack4(W_qkv_words, W_qkv_scales)
    qkv = y.reshape(B, N, 3, H, D).transpose(2, 0, 3, 1, 4)
    q, k, v = qkv[0], qkv[1], qkv[2]
    cos, sin = drofe_angles(D)
    demo = f64(demographic_info)
    age = demo[:, 0][:, None, None, None]
    gender = demo[:, 1][:, None, None, None]
    q = age * q * cos + gender * rotate_half(q) * sin
    k = age * k * cos + gender * rotate_half(k) * sin
    return q, k, v

@@ -1,0 +1,249 @@
+import math
+from contextlib import ExitStack
+
+import concourse.mybir as mybir
+from concourse.masks import make_identity
+
+F32 = mybir.dt.float32
+BF16 = mybir.dt.bfloat16
+I32 = mybir.dt.int32
+U32 = mybir.dt.uint32
+U8 = mybir.dt.uint8
+FP8X4 = mybir.dt.float8_e4m3fn_x4
+FP4X4 = mybir.dt.float4_e2m1fn_x4
+ALU = mybir.AluOpType
+ACT = mybir.ActivationFunctionType
+
+P = 128
+PACK = 4
+SAMPLES, TOKENS, K = 1024, 9, 1024
+HEADS, D = 2, 64
+PIECES = 3
+PASSES = K // (P * PACK)
+SAMPLE_TILES = SAMPLES // P
+BATCH = 3
+BATCHES = SAMPLE_TILES * TOKENS // BATCH
+LOADS_AHEAD = 8
+ROTATED = 2 * HEADS
+FREQS = D // 4
+BANDS = ((1, 4), (4, 8), (8, 10), (10, 12), (12, 30), (30, 45), (1, 8), (8, 30), (1, 45))
+
+FLOPS = 2 * SAMPLES * TOKENS * K * PIECES * P
+
+
+def build_rotary_tables(nc, pool, cos_tab, sin_tab):
+    steps_int = pool.tile([P, FREQS], I32)
+    nc.gpsimd.iota(steps_int[:], pattern=[[4, FREQS]], base=15, channel_multiplier=0)
+    steps = pool.tile([P, FREQS], F32)
+    nc.vector.tensor_copy(out=steps[:], in_=steps_int[:])
+
+    sixtieths = pool.tile([P, 2, TOKENS, 2, FREQS], F32)
+    for n in range(TOKENS):
+        for e in range(2):
+            nc.vector.tensor_scalar(
+                out=sixtieths[:, 1, n, e, :], in0=steps[:],
+                scalar1=float(2 * BANDS[n][e]), scalar2=None, op0=ALU.mult,
+            )
+    nc.vector.tensor_scalar(
+        out=sixtieths[:, 0], in0=sixtieths[:, 1], scalar1=15.0, scalar2=None, op0=ALU.add
+    )
+
+    half_turns_int = pool.tile([P, 2, TOKENS, 2, FREQS], I32)
+    nc.vector.tensor_scalar(
+        out=half_turns_int[:], in0=sixtieths[:], scalar1=1.0 / 30.0, scalar2=None, op0=ALU.mult
+    )
+    half_turns = pool.tile([P, 2, TOKENS, 2, FREQS], F32)
+    nc.vector.tensor_copy(out=half_turns[:], in_=half_turns_int[:])
+    rest = pool.tile([P, 2, TOKENS, 2, FREQS], F32)
+    nc.vector.scalar_tensor_tensor(
+        out=rest[:], in0=half_turns[:], scalar=-30.0, in1=sixtieths[:], op0=ALU.mult, op1=ALU.add
+    )
+    wave = pool.tile([P, 2, TOKENS, 2, FREQS], F32)
+    nc.scalar.activation(out=wave[:], in_=rest[:], func=ACT.Sin, scale=2.0 * math.pi / 60.0)
+
+    odd = pool.tile([P, 2, TOKENS, 2, FREQS], I32)
+    nc.vector.tensor_single_scalar(out=odd[:], in_=half_turns_int[:], scalar=1, op=ALU.bitwise_and)
+    sign = pool.tile([P, 2, TOKENS, 2, FREQS], F32)
+    nc.vector.tensor_scalar(
+        out=sign[:], in0=odd[:], scalar1=-2.0, scalar2=1.0, op0=ALU.mult, op1=ALU.add
+    )
+    nc.vector.tensor_tensor(out=wave[:], in0=wave[:], in1=sign[:], op=ALU.mult)
+
+    cos_wave = wave[:, 0].rearrange("p n e j -> p (n e j)").unsqueeze(2)
+    sin_wave = wave[:, 1].rearrange("p n e j -> p (n e j)").unsqueeze(2)
+    cos_pairs = cos_tab[:].rearrange("p n (c r) -> p (n c) r", r=2)
+    sin_pairs = sin_tab[:].rearrange("p n (c r) -> p (n c) r", r=2)
+    nc.vector.tensor_copy(out=cos_pairs, in_=cos_wave.to_broadcast([P, TOKENS * D // 2, 2]))
+    nc.vector.tensor_scalar(
+        out=sin_pairs[:, :, 0:1], in0=sin_wave, scalar1=-1.0, scalar2=None, op0=ALU.mult
+    )
+    nc.vector.tensor_copy(out=sin_pairs[:, :, 1:2], in_=sin_wave)
+
+
+def tile_xaiguiattention_pa_t_kernel(
+    tc, x, demographic_info, W_qkv_words, W_qkv_scales, out_0, out_1, out_2
+):
+    nc = tc.nc
+    x_rows = x.rearrange("(p t) n k -> p t n k", t=SAMPLE_TILES)
+    q_rows = out_0.rearrange("(p t) h n d -> p t (h n d)", t=SAMPLE_TILES)
+    k_rows = out_1.rearrange("(p t) h n d -> p t (h n d)", t=SAMPLE_TILES)
+    v_rows = out_2.rearrange("(p t) h n d -> p t (h n d)", t=SAMPLE_TILES)
+
+    with ExitStack() as ctx:
+        const = ctx.enter_context(tc.tile_pool(name="const", bufs=1))
+        x_pool = ctx.enter_context(tc.tile_pool(name="x", bufs=LOADS_AHEAD + 1))
+        grouped_pool = ctx.enter_context(tc.tile_pool(name="grouped", bufs=2 * BATCH))
+        code_pool = ctx.enter_context(tc.tile_pool(name="codes", bufs=2 * BATCH))
+        product_pool = ctx.enter_context(tc.tile_pool(name="products", bufs=2))
+        out_pool = ctx.enter_context(tc.tile_pool(name="out", bufs=2))
+        xt_psum = ctx.enter_context(tc.psum_pool(name="xt", bufs=BATCH))
+        qk_psum = ctx.enter_context(tc.psum_pool(name="qk", bufs=BATCH + 1))
+        v_psum = ctx.enter_context(tc.psum_pool(name="v", bufs=1))
+        ctx.enter_context(tc.manual_schedule())
+
+        x_tiles, grouped_tiles, code_tiles, qk_tiles, out_tiles = {}, {}, {}, {}, {}
+
+        def load(i):
+            t, n0 = i // (TOKENS // BATCH), BATCH * (i % (TOKENS // BATCH))
+            x_sb = x_pool.tile([P, BATCH, K], BF16)
+            nc.sync.dma_start(out=x_sb[:], in_=x_rows[:, t, n0 : n0 + BATCH, :])
+            x_tiles[i] = x_sb
+
+        def transpose(i):
+            grouped_tiles[i] = []
+            for u in range(BATCH):
+                words = x_tiles[i][:, u, :].bitcast(F32)
+                xt = xt_psum.tile([P, PASSES, 2, P], F32)
+                for g in range(PASSES):
+                    for s in range(2):
+                        nc.tensor.transpose(
+                            xt[:, g, s, :], words[:, 2 * P * g + s : 2 * P * (g + 1) : 2], identity[:]
+                        )
+                grouped = grouped_pool.tile([P, PASSES, P, PACK], BF16, align_bytes=64)
+                grouped_words = grouped[:].rearrange("p g r t -> p (g r t)").bitcast(F32)
+                nc.scalar.copy(
+                    out=grouped_words.rearrange("p (g r s) -> p g r s", g=PASSES, s=2),
+                    in_=xt[:].rearrange("p g s r -> p g r s"),
+                )
+                grouped_tiles[i].append(grouped)
+
+        def quantise(i):
+            code_tiles[i] = []
+            for u in range(BATCH):
+                codes = code_pool.tile([P, PASSES * P], U32, align_bytes=64)
+                scales = code_pool.tile([P, PASSES * P], U8, align_bytes=64)
+                nc.vector.quantize_mx(
+                    out=codes[:].bitcast(FP8X4),
+                    scales=scales[:],
+                    in_=grouped_tiles[i][u][:].rearrange("p g r t -> p (g r t)"),
+                )
+                code_tiles[i].append((codes, scales))
+
+        def multiply(i):
+            t, n0 = i // (TOKENS // BATCH), BATCH * (i % (TOKENS // BATCH))
+            if n0 == 0:
+                qk_out = out_pool.tile([P, ROTATED, TOKENS, D], F32)
+                v_out = out_pool.tile([P, HEADS, TOKENS, D], F32)
+                out_tiles[t] = (qk_out, v_out)
+            v_acc = v_psum.tile([P, BATCH, P], F32)
+            qk_tiles[i] = []
+            for u in range(BATCH):
+                codes, scales = code_tiles[i][u]
+                qk_acc = qk_psum.tile([P, 2 * P], F32)
+                for piece in range(PIECES):
+                    acc = qk_acc[:, P * piece : P * (piece + 1)] if piece < 2 else v_acc[:, u, :]
+                    for g in range(PASSES):
+                        nc.tensor.matmul_mx(
+                            out=acc,
+                            lhsT=codes[:, P * g : P * (g + 1)].bitcast(FP8X4),
+                            lhsT_scale=scales[:, P * g : P * (g + 1)],
+                            rhs=w_words[:, g, 2 * P * piece : 2 * P * (piece + 1)].bitcast(FP4X4),
+                            rhs_scale=w_scales[:, g, P * piece : P * (piece + 1)],
+                            start=(g == 0),
+                            stop=(g == PASSES - 1),
+                        )
+                qk_tiles[i].append(qk_acc)
+            nc.scalar.copy(
+                out=out_tiles[t][1][:, :, n0 : n0 + BATCH, :],
+                in_=v_acc[:].rearrange("p u (h d) -> p h u d", h=HEADS),
+            )
+
+        def rotate(i):
+            t, n0 = i // (TOKENS // BATCH), BATCH * (i % (TOKENS // BATCH))
+            qk_out, v_out = out_tiles[t]
+            cos_part = product_pool.tile([P, ROTATED, BATCH, D], F32)
+            sin_part = product_pool.tile([P, ROTATED, BATCH, D], F32)
+            for u in range(BATCH):
+                y = qk_tiles[i][u]
+                nc.vector.scalar_tensor_tensor(
+                    out=cos_part[:, :, u, :],
+                    in0=y[:].rearrange("p (a d) -> p a d", d=D),
+                    scalar=demo[:, t, 0:1],
+                    in1=cos_tab[:, n0 + u, :].unsqueeze(1).to_broadcast([P, ROTATED, D]),
+                    op0=ALU.mult,
+                    op1=ALU.mult,
+                )
+                nc.vector.scalar_tensor_tensor(
+                    out=sin_part[:, :, u, :].rearrange("p a (j r) -> p a j r", r=2),
+                    in0=y[:].rearrange("p (a j r) -> p a j r", a=ROTATED, r=2)[:, :, :, ::-1],
+                    scalar=demo[:, t, 1:2],
+                    in1=sin_tab[:, n0 + u, :]
+                    .rearrange("p (j r) -> p j r", r=2)
+                    .unsqueeze(1)
+                    .to_broadcast([P, ROTATED, D // 2, 2]),
+                    op0=ALU.mult,
+                    op1=ALU.mult,
+                )
+            nc.gpsimd.tensor_tensor(
+                out=qk_out[:, :, n0 : n0 + BATCH, :], in0=cos_part[:], in1=sin_part[:], op=ALU.add
+            )
+            if n0 + BATCH == TOKENS:
+                nc.sync.dma_start(
+                    out=q_rows[:, t, :], in_=qk_out[:, 0:HEADS].rearrange("p a n d -> p (a n d)")
+                )
+                nc.sync.dma_start(
+                    out=k_rows[:, t, :], in_=qk_out[:, HEADS:ROTATED].rearrange("p a n d -> p (a n d)")
+                )
+                nc.sync.dma_start(out=v_rows[:, t, :], in_=v_out[:].rearrange("p h n d -> p (h n d)"))
+
+        w_words = const.tile([P, PASSES, 2 * PIECES * P], U8, align_bytes=64)
+        w_scales = const.tile([P, PASSES, PIECES * P], U8, align_bytes=64)
+        nc.vector.memset(w_scales[:].rearrange("p g c -> p (g c)").bitcast(I32), 0)
+        load(0)
+        nc.sync.dma_start(
+            out=w_words[:].bitcast(I32), in_=W_qkv_words.rearrange("g p c -> p g c").bitcast(I32)
+        )
+        scale_rows = W_qkv_scales.rearrange("g q c -> q g c")
+        for quadrant in range(4):
+            nc.sync.dma_start(
+                out=w_scales[32 * quadrant : 32 * quadrant + 4].bitcast(I32),
+                in_=scale_rows[4 * quadrant : 4 * quadrant + 4].bitcast(I32),
+            )
+        demo_bf16 = const.tile([P, SAMPLE_TILES, 2], BF16)
+        nc.sync.dma_start(
+            out=demo_bf16[:], in_=demographic_info.rearrange("(p t) c -> p t c", t=SAMPLE_TILES)
+        )
+        for i in range(1, LOADS_AHEAD):
+            load(i)
+
+        identity = const.tile([P, P], F32)
+        make_identity(nc, identity[:])
+        cos_tab = const.tile([P, TOKENS, D], F32)
+        sin_tab = const.tile([P, TOKENS, D], F32)
+        build_rotary_tables(nc, const, cos_tab, sin_tab)
+        demo = const.tile([P, SAMPLE_TILES, 2], F32)
+        nc.gpsimd.tensor_copy(out=demo[:], in_=demo_bf16[:])
+
+        transpose(0)
+        quantise(0)
+        for i in range(BATCHES + 1):
+            if i + 1 < BATCHES:
+                transpose(i + 1)
+            if i >= 1:
+                rotate(i - 1)
+            if i + 1 < BATCHES:
+                quantise(i + 1)
+            if i < BATCHES:
+                multiply(i)
+            if i + LOADS_AHEAD < BATCHES:
+                load(i + LOADS_AHEAD)

@@ -21,9 +21,12 @@ HEADS, D = 2, 64
 PIECES = 3
 PASSES = K // (P * PACK)
 SAMPLE_TILES = SAMPLES // P
-BATCH = 3
-BATCHES = SAMPLE_TILES * TOKENS // BATCH
+UNITS = SAMPLE_TILES * TOKENS
+CHUNK = 3
+CHUNKS = UNITS // CHUNK
 LOADS_AHEAD = 8
+RUN = 3
+RUNS = UNITS // RUN
 ROTATED = 2 * HEADS
 FREQS = D // 4
 BANDS = ((1, 4), (4, 8), (8, 10), (10, 12), (12, 30), (30, 45), (1, 8), (8, 30), (1, 45))
@@ -85,34 +88,43 @@ def tile_xaiguiattention_pa_t_kernel(
 ):
     nc = tc.nc
     x_rows = x.rearrange("(p t) n k -> p t n k", t=SAMPLE_TILES)
-    q_rows = out_0.rearrange("(p t) h n d -> p t (h n d)", t=SAMPLE_TILES)
-    k_rows = out_1.rearrange("(p t) h n d -> p t (h n d)", t=SAMPLE_TILES)
-    v_rows = out_2.rearrange("(p t) h n d -> p t (h n d)", t=SAMPLE_TILES)
+    q_rows = out_0.rearrange("(p t) h n d -> p t h n d", t=SAMPLE_TILES)
+    k_rows = out_1.rearrange("(p t) h n d -> p t h n d", t=SAMPLE_TILES)
+    v_rows = out_2.rearrange("(p t) h n d -> p t h n d", t=SAMPLE_TILES)
 
     with ExitStack() as ctx:
         const = ctx.enter_context(tc.tile_pool(name="const", bufs=1))
         x_pool = ctx.enter_context(tc.tile_pool(name="x", bufs=LOADS_AHEAD + 1))
-        grouped_pool = ctx.enter_context(tc.tile_pool(name="grouped", bufs=2 * BATCH))
-        code_pool = ctx.enter_context(tc.tile_pool(name="codes", bufs=2 * BATCH))
-        product_pool = ctx.enter_context(tc.tile_pool(name="products", bufs=2))
+        grouped_pool = ctx.enter_context(tc.tile_pool(name="grouped", bufs=2 * RUN))
+        code_pool = ctx.enter_context(tc.tile_pool(name="codes", bufs=2 * RUN))
+        product_pool = ctx.enter_context(tc.tile_pool(name="products", bufs=2 * RUN))
         out_pool = ctx.enter_context(tc.tile_pool(name="out", bufs=2))
-        xt_psum = ctx.enter_context(tc.psum_pool(name="xt", bufs=BATCH))
-        qk_psum = ctx.enter_context(tc.psum_pool(name="qk", bufs=BATCH + 1))
+        xt_psum = ctx.enter_context(tc.psum_pool(name="xt", bufs=3))
+        qk_psum = ctx.enter_context(tc.psum_pool(name="qk", bufs=4))
         v_psum = ctx.enter_context(tc.psum_pool(name="v", bufs=1))
         ctx.enter_context(tc.manual_schedule())
 
         x_tiles, grouped_tiles, code_tiles, qk_tiles, out_tiles = {}, {}, {}, {}, {}
 
-        def load(i):
-            t, n0 = i // (TOKENS // BATCH), BATCH * (i % (TOKENS // BATCH))
-            x_sb = x_pool.tile([P, BATCH, K], BF16)
-            nc.sync.dma_start(out=x_sb[:], in_=x_rows[:, t, n0 : n0 + BATCH, :])
-            x_tiles[i] = x_sb
+        def units_of(run):
+            return range(RUN * run, RUN * (run + 1))
 
-        def transpose(i):
-            grouped_tiles[i] = []
-            for u in range(BATCH):
-                words = x_tiles[i][:, u, :].bitcast(F32)
+        def load(chunk):
+            t, n0 = (CHUNK * chunk) // TOKENS, (CHUNK * chunk) % TOKENS
+            x_sb = x_pool.tile([P, CHUNK, K], BF16)
+            tokens = 1 if chunk == 0 else CHUNK
+            for u in range(0, CHUNK, tokens):
+                nc.sync.dma_start(
+                    out=x_sb[:, u : u + tokens, :], in_=x_rows[:, t, n0 + u : n0 + u + tokens, :]
+                )
+            x_tiles[chunk] = x_sb
+
+        def transpose(run):
+            for unit in units_of(run):
+                chunk, u = unit // CHUNK, unit % CHUNK
+                if u == 0 and chunk + LOADS_AHEAD < CHUNKS:
+                    load(chunk + LOADS_AHEAD)
+                words = x_tiles[chunk][:, u, :].bitcast(F32)
                 xt = xt_psum.tile([P, PASSES, 2, P], F32)
                 for g in range(PASSES):
                     for s in range(2):
@@ -125,86 +137,89 @@ def tile_xaiguiattention_pa_t_kernel(
                     out=grouped_words.rearrange("p (g r s) -> p g r s", g=PASSES, s=2),
                     in_=xt[:].rearrange("p g s r -> p g r s"),
                 )
-                grouped_tiles[i].append(grouped)
+                grouped_tiles[unit] = grouped
 
-        def quantise(i):
-            code_tiles[i] = []
-            for u in range(BATCH):
+        def quantise(run):
+            for unit in units_of(run):
                 codes = code_pool.tile([P, PASSES * P], U32, align_bytes=64)
                 scales = code_pool.tile([P, PASSES * P], U8, align_bytes=64)
                 nc.vector.quantize_mx(
                     out=codes[:].bitcast(FP8X4),
                     scales=scales[:],
-                    in_=grouped_tiles[i][u][:].rearrange("p g r t -> p (g r t)"),
+                    in_=grouped_tiles[unit][:].rearrange("p g r t -> p (g r t)"),
                 )
-                code_tiles[i].append((codes, scales))
+                code_tiles[unit] = (codes, scales)
 
-        def multiply(i):
-            t, n0 = i // (TOKENS // BATCH), BATCH * (i % (TOKENS // BATCH))
-            if n0 == 0:
-                qk_out = out_pool.tile([P, ROTATED, TOKENS, D], F32)
-                v_out = out_pool.tile([P, HEADS, TOKENS, D], F32)
-                out_tiles[t] = (qk_out, v_out)
-            v_acc = v_psum.tile([P, BATCH, P], F32)
-            qk_tiles[i] = []
-            for u in range(BATCH):
-                codes, scales = code_tiles[i][u]
+        def multiply_piece(acc, unit, piece):
+            codes, scales = code_tiles[unit]
+            for g in range(PASSES):
+                nc.tensor.matmul_mx(
+                    out=acc,
+                    lhsT=codes[:, P * g : P * (g + 1)].bitcast(FP8X4),
+                    lhsT_scale=scales[:, P * g : P * (g + 1)],
+                    rhs=w_words[:, g, 2 * P * piece : 2 * P * (piece + 1)].bitcast(FP4X4),
+                    rhs_scale=w_scales[:, g, P * piece : P * (piece + 1)],
+                    start=(g == 0),
+                    stop=(g == PASSES - 1),
+                )
+
+        def multiply(run):
+            for unit in units_of(run):
                 qk_acc = qk_psum.tile([P, 2 * P], F32)
-                for piece in range(PIECES):
-                    acc = qk_acc[:, P * piece : P * (piece + 1)] if piece < 2 else v_acc[:, u, :]
-                    for g in range(PASSES):
-                        nc.tensor.matmul_mx(
-                            out=acc,
-                            lhsT=codes[:, P * g : P * (g + 1)].bitcast(FP8X4),
-                            lhsT_scale=scales[:, P * g : P * (g + 1)],
-                            rhs=w_words[:, g, 2 * P * piece : 2 * P * (piece + 1)].bitcast(FP4X4),
-                            rhs_scale=w_scales[:, g, P * piece : P * (piece + 1)],
-                            start=(g == 0),
-                            stop=(g == PASSES - 1),
-                        )
-                qk_tiles[i].append(qk_acc)
-            nc.scalar.copy(
-                out=out_tiles[t][1][:, :, n0 : n0 + BATCH, :],
-                in_=v_acc[:].rearrange("p u (h d) -> p h u d", h=HEADS),
-            )
+                multiply_piece(qk_acc[:, 0:P], unit, 0)
+                multiply_piece(qk_acc[:, P : 2 * P], unit, 1)
+                qk_tiles[unit] = qk_acc
+            v_acc = v_psum.tile([P, RUN, P], F32)
+            for unit in units_of(run):
+                multiply_piece(v_acc[:, unit % RUN, :], unit, 2)
+            for unit in units_of(run):
+                t, n = unit // TOKENS, unit % TOKENS
+                if n == 0:
+                    qk_out = out_pool.tile([P, ROTATED, TOKENS, D], F32)
+                    v_out = out_pool.tile([P, HEADS, TOKENS, D], F32)
+                    out_tiles[t] = (qk_out, v_out)
+                nc.scalar.copy(
+                    out=out_tiles[t][1][:, :, n, :],
+                    in_=v_acc[:, unit % RUN, :].rearrange("p (h d) -> p h d", h=HEADS),
+                )
 
-        def rotate(i):
-            t, n0 = i // (TOKENS // BATCH), BATCH * (i % (TOKENS // BATCH))
-            qk_out, v_out = out_tiles[t]
-            cos_part = product_pool.tile([P, ROTATED, BATCH, D], F32)
-            sin_part = product_pool.tile([P, ROTATED, BATCH, D], F32)
-            for u in range(BATCH):
-                y = qk_tiles[i][u]
+        def rotate(run):
+            for unit in units_of(run):
+                t, n = unit // TOKENS, unit % TOKENS
+                qk_out, v_out = out_tiles[t]
+                y = qk_tiles[unit]
+                cos_part = product_pool.tile([P, ROTATED, D], F32)
+                sin_part = product_pool.tile([P, ROTATED, D], F32)
                 nc.vector.scalar_tensor_tensor(
-                    out=cos_part[:, :, u, :],
+                    out=cos_part[:],
                     in0=y[:].rearrange("p (a d) -> p a d", d=D),
                     scalar=demo[:, t, 0:1],
-                    in1=cos_tab[:, n0 + u, :].unsqueeze(1).to_broadcast([P, ROTATED, D]),
+                    in1=cos_tab[:, n, :].unsqueeze(1).to_broadcast([P, ROTATED, D]),
                     op0=ALU.mult,
                     op1=ALU.mult,
                 )
                 nc.vector.scalar_tensor_tensor(
-                    out=sin_part[:, :, u, :].rearrange("p a (j r) -> p a j r", r=2),
+                    out=sin_part[:].rearrange("p a (j r) -> p a j r", r=2),
                     in0=y[:].rearrange("p (a j r) -> p a j r", a=ROTATED, r=2)[:, :, :, ::-1],
                     scalar=demo[:, t, 1:2],
-                    in1=sin_tab[:, n0 + u, :]
+                    in1=sin_tab[:, n, :]
                     .rearrange("p (j r) -> p j r", r=2)
                     .unsqueeze(1)
                     .to_broadcast([P, ROTATED, D // 2, 2]),
                     op0=ALU.mult,
                     op1=ALU.mult,
                 )
-            nc.gpsimd.tensor_tensor(
-                out=qk_out[:, :, n0 : n0 + BATCH, :], in0=cos_part[:], in1=sin_part[:], op=ALU.add
-            )
-            if n0 + BATCH == TOKENS:
-                nc.sync.dma_start(
-                    out=q_rows[:, t, :], in_=qk_out[:, 0:HEADS].rearrange("p a n d -> p (a n d)")
+                nc.gpsimd.tensor_tensor(
+                    out=qk_out[:, :, n, :], in0=cos_part[:], in1=sin_part[:], op=ALU.add
                 )
-                nc.sync.dma_start(
-                    out=k_rows[:, t, :], in_=qk_out[:, HEADS:ROTATED].rearrange("p a n d -> p (a n d)")
-                )
-                nc.sync.dma_start(out=v_rows[:, t, :], in_=v_out[:].rearrange("p h n d -> p (h n d)"))
+                tokens = CHUNK if t == SAMPLE_TILES - 1 else TOKENS
+                if (n + 1) % tokens == 0:
+                    done = slice(n + 1 - tokens, n + 1)
+                    nc.sync.dma_start(out=v_rows[:, t, :, done, :], in_=v_out[:, :, done, :])
+                    nc.sync.dma_start(out=q_rows[:, t, :, done, :], in_=qk_out[:, 0:HEADS, done, :])
+                    nc.sync.dma_start(
+                        out=k_rows[:, t, :, done, :], in_=qk_out[:, HEADS:ROTATED, done, :]
+                    )
 
         w_words = const.tile([P, PASSES, 2 * PIECES * P], U8, align_bytes=64)
         w_scales = const.tile([P, PASSES, PIECES * P], U8, align_bytes=64)
@@ -223,8 +238,8 @@ def tile_xaiguiattention_pa_t_kernel(
         nc.sync.dma_start(
             out=demo_bf16[:], in_=demographic_info.rearrange("(p t) c -> p t c", t=SAMPLE_TILES)
         )
-        for i in range(1, LOADS_AHEAD):
-            load(i)
+        for chunk in range(1, LOADS_AHEAD):
+            load(chunk)
 
         identity = const.tile([P, P], F32)
         make_identity(nc, identity[:])
@@ -236,14 +251,12 @@ def tile_xaiguiattention_pa_t_kernel(
 
         transpose(0)
         quantise(0)
-        for i in range(BATCHES + 1):
-            if i + 1 < BATCHES:
-                transpose(i + 1)
-            if i >= 1:
-                rotate(i - 1)
-            if i + 1 < BATCHES:
-                quantise(i + 1)
-            if i < BATCHES:
-                multiply(i)
-            if i + LOADS_AHEAD < BATCHES:
-                load(i + LOADS_AHEAD)
+        for run in range(RUNS + 1):
+            if run + 1 < RUNS:
+                transpose(run + 1)
+            if run >= 1:
+                rotate(run - 1)
+            if run + 1 < RUNS:
+                quantise(run + 1)
+            if run < RUNS:
+                multiply(run)

@@ -27,6 +27,7 @@ CHUNKS = UNITS // CHUNK
 LOADS_AHEAD = 8
 RUN = 3
 RUNS = UNITS // RUN
+VECTOR_ADDS = 2
 ROTATED = 2 * HEADS
 FREQS = D // 4
 BANDS = ((1, 4), (4, 8), (8, 10), (10, 12), (12, 30), (30, 45), (1, 8), (8, 30), (1, 45))
@@ -112,7 +113,7 @@ def tile_xaiguiattention_pa_t_kernel(
         def load(chunk):
             t, n0 = (CHUNK * chunk) // TOKENS, (CHUNK * chunk) % TOKENS
             x_sb = x_pool.tile([P, CHUNK, K], BF16)
-            tokens = 1 if chunk == 0 else CHUNK
+            tokens = 1 if chunk <= 1 else CHUNK
             for u in range(0, CHUNK, tokens):
                 nc.sync.dma_start(
                     out=x_sb[:, u : u + tokens, :], in_=x_rows[:, t, n0 + u : n0 + u + tokens, :]
@@ -209,7 +210,8 @@ def tile_xaiguiattention_pa_t_kernel(
                     op0=ALU.mult,
                     op1=ALU.mult,
                 )
-                nc.gpsimd.tensor_tensor(
+                adder = nc.vector if unit >= UNITS - VECTOR_ADDS else nc.gpsimd
+                adder.tensor_tensor(
                     out=qk_out[:, :, n, :], in0=cos_part[:], in1=sin_part[:], op=ALU.add
                 )
                 tokens = CHUNK if t == SAMPLE_TILES - 1 else TOKENS
@@ -225,6 +227,7 @@ def tile_xaiguiattention_pa_t_kernel(
         w_scales = const.tile([P, PASSES, PIECES * P], U8, align_bytes=64)
         nc.vector.memset(w_scales[:].rearrange("p g c -> p (g c)").bitcast(I32), 0)
         load(0)
+        load(1)
         nc.sync.dma_start(
             out=w_words[:].bitcast(I32), in_=W_qkv_words.rearrange("g p c -> p g c").bitcast(I32)
         )
@@ -238,7 +241,7 @@ def tile_xaiguiattention_pa_t_kernel(
         nc.sync.dma_start(
             out=demo_bf16[:], in_=demographic_info.rearrange("(p t) c -> p t c", t=SAMPLE_TILES)
         )
-        for chunk in range(1, LOADS_AHEAD):
+        for chunk in range(2, LOADS_AHEAD):
             load(chunk)
 
         identity = const.tile([P, P], F32)

import math
from contextlib import ExitStack

import concourse.mybir as mybir
from concourse.masks import make_identity

F32 = mybir.dt.float32
BF16 = mybir.dt.bfloat16
I32 = mybir.dt.int32
U32 = mybir.dt.uint32
U8 = mybir.dt.uint8
FP8X4 = mybir.dt.float8_e4m3fn_x4
FP4X4 = mybir.dt.float4_e2m1fn_x4
ALU = mybir.AluOpType
ACT = mybir.ActivationFunctionType

P = 128
PACK = 4
SAMPLES, TOKENS, K = 1024, 9, 1024
HEADS, D = 2, 64
PIECES = 3
PASSES = K // (P * PACK)
SAMPLE_TILES = SAMPLES // P
UNITS = SAMPLE_TILES * TOKENS
CHUNK = 3
CHUNKS = UNITS // CHUNK
LOADS_AHEAD = 8
RUN = 3
RUNS = UNITS // RUN
VECTOR_ADDS = 2
ROTATED = 2 * HEADS
FREQS = D // 4
BANDS = ((1, 4), (4, 8), (8, 10), (10, 12), (12, 30), (30, 45), (1, 8), (8, 30), (1, 45))

FLOPS = 2 * SAMPLES * TOKENS * K * PIECES * P


def build_rotary_tables(nc, pool, cos_tab, sin_tab):
    steps_int = pool.tile([P, FREQS], I32)
    nc.gpsimd.iota(steps_int[:], pattern=[[4, FREQS]], base=15, channel_multiplier=0)
    steps = pool.tile([P, FREQS], F32)
    nc.vector.tensor_copy(out=steps[:], in_=steps_int[:])

    sixtieths = pool.tile([P, 2, TOKENS, 2, FREQS], F32)
    for n in range(TOKENS):
        for e in range(2):
            nc.vector.tensor_scalar(
                out=sixtieths[:, 1, n, e, :], in0=steps[:],
                scalar1=float(2 * BANDS[n][e]), scalar2=None, op0=ALU.mult,
            )
    nc.vector.tensor_scalar(
        out=sixtieths[:, 0], in0=sixtieths[:, 1], scalar1=15.0, scalar2=None, op0=ALU.add
    )

    half_turns_int = pool.tile([P, 2, TOKENS, 2, FREQS], I32)
    nc.vector.tensor_scalar(
        out=half_turns_int[:], in0=sixtieths[:], scalar1=1.0 / 30.0, scalar2=None, op0=ALU.mult
    )
    half_turns = pool.tile([P, 2, TOKENS, 2, FREQS], F32)
    nc.vector.tensor_copy(out=half_turns[:], in_=half_turns_int[:])
    rest = pool.tile([P, 2, TOKENS, 2, FREQS], F32)
    nc.vector.scalar_tensor_tensor(
        out=rest[:], in0=half_turns[:], scalar=-30.0, in1=sixtieths[:], op0=ALU.mult, op1=ALU.add
    )
    wave = pool.tile([P, 2, TOKENS, 2, FREQS], F32)
    nc.scalar.activation(out=wave[:], in_=rest[:], func=ACT.Sin, scale=2.0 * math.pi / 60.0)

    odd = pool.tile([P, 2, TOKENS, 2, FREQS], I32)
    nc.vector.tensor_single_scalar(out=odd[:], in_=half_turns_int[:], scalar=1, op=ALU.bitwise_and)
    sign = pool.tile([P, 2, TOKENS, 2, FREQS], F32)
    nc.vector.tensor_scalar(
        out=sign[:], in0=odd[:], scalar1=-2.0, scalar2=1.0, op0=ALU.mult, op1=ALU.add
    )
    nc.vector.tensor_tensor(out=wave[:], in0=wave[:], in1=sign[:], op=ALU.mult)

    cos_wave = wave[:, 0].rearrange("p n e j -> p (n e j)").unsqueeze(2)
    sin_wave = wave[:, 1].rearrange("p n e j -> p (n e j)").unsqueeze(2)
    cos_pairs = cos_tab[:].rearrange("p n (c r) -> p (n c) r", r=2)
    sin_pairs = sin_tab[:].rearrange("p n (c r) -> p (n c) r", r=2)
    nc.vector.tensor_copy(out=cos_pairs, in_=cos_wave.to_broadcast([P, TOKENS * D // 2, 2]))
    nc.vector.tensor_scalar(
        out=sin_pairs[:, :, 0:1], in0=sin_wave, scalar1=-1.0, scalar2=None, op0=ALU.mult
    )
    nc.vector.tensor_copy(out=sin_pairs[:, :, 1:2], in_=sin_wave)


def tile_xaiguiattention_pa_t_kernel(
    tc, x, demographic_info, W_qkv_words, W_qkv_scales, out_0, out_1, out_2
):
    nc = tc.nc
    x_rows = x.rearrange("(p t) n k -> p t n k", t=SAMPLE_TILES)
    q_rows = out_0.rearrange("(p t) h n d -> p t h n d", t=SAMPLE_TILES)
    k_rows = out_1.rearrange("(p t) h n d -> p t h n d", t=SAMPLE_TILES)
    v_rows = out_2.rearrange("(p t) h n d -> p t h n d", t=SAMPLE_TILES)

    with ExitStack() as ctx:
        const = ctx.enter_context(tc.tile_pool(name="const", bufs=1))
        x_pool = ctx.enter_context(tc.tile_pool(name="x", bufs=LOADS_AHEAD + 1))
        grouped_pool = ctx.enter_context(tc.tile_pool(name="grouped", bufs=2 * RUN))
        code_pool = ctx.enter_context(tc.tile_pool(name="codes", bufs=2 * RUN))
        product_pool = ctx.enter_context(tc.tile_pool(name="products", bufs=2 * RUN))
        out_pool = ctx.enter_context(tc.tile_pool(name="out", bufs=2))
        xt_psum = ctx.enter_context(tc.psum_pool(name="xt", bufs=3))
        qk_psum = ctx.enter_context(tc.psum_pool(name="qk", bufs=4))
        v_psum = ctx.enter_context(tc.psum_pool(name="v", bufs=1))
        ctx.enter_context(tc.manual_schedule())

        x_tiles, grouped_tiles, code_tiles, qk_tiles, out_tiles = {}, {}, {}, {}, {}

        def units_of(run):
            return range(RUN * run, RUN * (run + 1))

        def load(chunk):
            t, n0 = (CHUNK * chunk) // TOKENS, (CHUNK * chunk) % TOKENS
            x_sb = x_pool.tile([P, CHUNK, K], BF16)
            tokens = 1 if chunk <= 1 else CHUNK
            for u in range(0, CHUNK, tokens):
                nc.sync.dma_start(
                    out=x_sb[:, u : u + tokens, :], in_=x_rows[:, t, n0 + u : n0 + u + tokens, :]
                )
            x_tiles[chunk] = x_sb

        def transpose(run):
            for unit in units_of(run):
                chunk, u = unit // CHUNK, unit % CHUNK
                if u == 0 and chunk + LOADS_AHEAD < CHUNKS:
                    load(chunk + LOADS_AHEAD)
                words = x_tiles[chunk][:, u, :].bitcast(F32)
                xt = xt_psum.tile([P, PASSES, 2, P], F32)
                for g in range(PASSES):
                    for s in range(2):
                        nc.tensor.transpose(
                            xt[:, g, s, :], words[:, 2 * P * g + s : 2 * P * (g + 1) : 2], identity[:]
                        )
                grouped = grouped_pool.tile([P, PASSES, P, PACK], BF16, align_bytes=64)
                grouped_words = grouped[:].rearrange("p g r t -> p (g r t)").bitcast(F32)
                nc.scalar.copy(
                    out=grouped_words.rearrange("p (g r s) -> p g r s", g=PASSES, s=2),
                    in_=xt[:].rearrange("p g s r -> p g r s"),
                )
                grouped_tiles[unit] = grouped

        def quantise(run):
            for unit in units_of(run):
                codes = code_pool.tile([P, PASSES * P], U32, align_bytes=64)
                scales = code_pool.tile([P, PASSES * P], U8, align_bytes=64)
                nc.vector.quantize_mx(
                    out=codes[:].bitcast(FP8X4),
                    scales=scales[:],
                    in_=grouped_tiles[unit][:].rearrange("p g r t -> p (g r t)"),
                )
                code_tiles[unit] = (codes, scales)

        def multiply_piece(acc, unit, piece):
            codes, scales = code_tiles[unit]
            for g in range(PASSES):
                nc.tensor.matmul_mx(
                    out=acc,
                    lhsT=codes[:, P * g : P * (g + 1)].bitcast(FP8X4),
                    lhsT_scale=scales[:, P * g : P * (g + 1)],
                    rhs=w_words[:, g, 2 * P * piece : 2 * P * (piece + 1)].bitcast(FP4X4),
                    rhs_scale=w_scales[:, g, P * piece : P * (piece + 1)],
                    start=(g == 0),
                    stop=(g == PASSES - 1),
                )

        def multiply(run):
            for unit in units_of(run):
                qk_acc = qk_psum.tile([P, 2 * P], F32)
                multiply_piece(qk_acc[:, 0:P], unit, 0)
                multiply_piece(qk_acc[:, P : 2 * P], unit, 1)
                qk_tiles[unit] = qk_acc
            v_acc = v_psum.tile([P, RUN, P], F32)
            for unit in units_of(run):
                multiply_piece(v_acc[:, unit % RUN, :], unit, 2)
            for unit in units_of(run):
                t, n = unit // TOKENS, unit % TOKENS
                if n == 0:
                    qk_out = out_pool.tile([P, ROTATED, TOKENS, D], F32)
                    v_out = out_pool.tile([P, HEADS, TOKENS, D], F32)
                    out_tiles[t] = (qk_out, v_out)
                nc.scalar.copy(
                    out=out_tiles[t][1][:, :, n, :],
                    in_=v_acc[:, unit % RUN, :].rearrange("p (h d) -> p h d", h=HEADS),
                )

        def rotate(run):
            for unit in units_of(run):
                t, n = unit // TOKENS, unit % TOKENS
                qk_out, v_out = out_tiles[t]
                y = qk_tiles[unit]
                cos_part = product_pool.tile([P, ROTATED, D], F32)
                sin_part = product_pool.tile([P, ROTATED, D], F32)
                nc.vector.scalar_tensor_tensor(
                    out=cos_part[:],
                    in0=y[:].rearrange("p (a d) -> p a d", d=D),
                    scalar=demo[:, t, 0:1],
                    in1=cos_tab[:, n, :].unsqueeze(1).to_broadcast([P, ROTATED, D]),
                    op0=ALU.mult,
                    op1=ALU.mult,
                )
                nc.vector.scalar_tensor_tensor(
                    out=sin_part[:].rearrange("p a (j r) -> p a j r", r=2),
                    in0=y[:].rearrange("p (a j r) -> p a j r", a=ROTATED, r=2)[:, :, :, ::-1],
                    scalar=demo[:, t, 1:2],
                    in1=sin_tab[:, n, :]
                    .rearrange("p (j r) -> p j r", r=2)
                    .unsqueeze(1)
                    .to_broadcast([P, ROTATED, D // 2, 2]),
                    op0=ALU.mult,
                    op1=ALU.mult,
                )
                adder = nc.vector if unit >= UNITS - VECTOR_ADDS else nc.gpsimd
                adder.tensor_tensor(
                    out=qk_out[:, :, n, :], in0=cos_part[:], in1=sin_part[:], op=ALU.add
                )
                tokens = CHUNK if t == SAMPLE_TILES - 1 else TOKENS
                if (n + 1) % tokens == 0:
                    done = slice(n + 1 - tokens, n + 1)
                    nc.sync.dma_start(out=v_rows[:, t, :, done, :], in_=v_out[:, :, done, :])
                    nc.sync.dma_start(out=q_rows[:, t, :, done, :], in_=qk_out[:, 0:HEADS, done, :])
                    nc.sync.dma_start(
                        out=k_rows[:, t, :, done, :], in_=qk_out[:, HEADS:ROTATED, done, :]
                    )

        w_words = const.tile([P, PASSES, 2 * PIECES * P], U8, align_bytes=64)
        w_scales = const.tile([P, PASSES, PIECES * P], U8, align_bytes=64)
        nc.vector.memset(w_scales[:].rearrange("p g c -> p (g c)").bitcast(I32), 0)
        load(0)
        load(1)
        nc.sync.dma_start(
            out=w_words[:].bitcast(I32), in_=W_qkv_words.rearrange("g p c -> p g c").bitcast(I32)
        )
        scale_rows = W_qkv_scales.rearrange("g q c -> q g c")
        for quadrant in range(4):
            nc.sync.dma_start(
                out=w_scales[32 * quadrant : 32 * quadrant + 4].bitcast(I32),
                in_=scale_rows[4 * quadrant : 4 * quadrant + 4].bitcast(I32),
            )
        demo_bf16 = const.tile([P, SAMPLE_TILES, 2], BF16)
        nc.sync.dma_start(
            out=demo_bf16[:], in_=demographic_info.rearrange("(p t) c -> p t c", t=SAMPLE_TILES)
        )
        for chunk in range(2, LOADS_AHEAD):
            load(chunk)

        identity = const.tile([P, P], F32)
        make_identity(nc, identity[:])
        cos_tab = const.tile([P, TOKENS, D], F32)
        sin_tab = const.tile([P, TOKENS, D], F32)
        build_rotary_tables(nc, const, cos_tab, sin_tab)
        demo = const.tile([P, SAMPLE_TILES, 2], F32)
        nc.gpsimd.tensor_copy(out=demo[:], in_=demo_bf16[:])

        transpose(0)
        quantise(0)
        for run in range(RUNS + 1):
            if run + 1 < RUNS:
                transpose(run + 1)
            if run >= 1:
                rotate(run - 1)
            if run + 1 < RUNS:
                quantise(run + 1)
            if run < RUNS:
                multiply(run)
